import numpy as np
import ml_dtypes


def mxq(x, axis, fmt="e4m3"):
    dtype, down = {"e4m3": (ml_dtypes.float8_e4m3fn, 7), "e5m2": (ml_dtypes.float8_e5m2, 14)}[fmt]
    v = np.moveaxis(np.asarray(x, np.float32).astype(ml_dtypes.bfloat16).astype(np.float64), axis, -1)
    blocks = v.reshape(v.shape[:-1] + (-1, 32))
    amax = np.abs(blocks).max(-1, keepdims=True)
    byte = np.maximum(np.where(amax > 0, np.frexp(amax)[1] - 1 + 127, 0) - down, 1)
    scale = np.exp2(byte - 127.0)
    codes = (blocks / scale).astype(np.float32).astype(dtype).astype(np.float64)
    return np.moveaxis((codes * scale).reshape(v.shape), -1, axis)


WIDE = False


def mx_kscale(k):
    if not WIDE:
        return np.ones(k)
    levels = np.array([10, -10, 5, -5, 0])
    if k % 512:
        return np.exp2(np.random.permutation(np.resize(levels, k // 32))).repeat(32)
    a = np.empty((k // 512, 16))
    for p in range(k // 512):
        a[p, :8] = np.random.permutation(np.resize(levels, 8))
        for g in range(8):
            far = levels[np.abs(levels - a[p, g]) >= 10]
            a[p, g + 8] = far[np.random.randint(len(far))]
    return np.exp2(a.ravel()).repeat(32)


BF16 = ml_dtypes.bfloat16


def bf(x):
    return np.asarray(x, np.float32).astype(BF16)


def f64(x):
    return np.asarray(x).astype(np.float64)


B, S, DIM, N_HEADS, Q_LORA, KV_LORA, NOPE, ROPE, V_HEAD = 1, 512, 2048, 16, 1536, 512, 128, 64, 128
HV = N_HEADS * V_HEAD


def setup_inputs():
    s, t = mx_kscale(KV_LORA), mx_kscale(HV)
    return {"o_lat": bf(np.random.standard_normal((B, S, N_HEADS, KV_LORA)) * 0.35 * s),
            "w_uv": bf(np.random.standard_normal((N_HEADS, V_HEAD, KV_LORA)) * 2.0 / np.sqrt(KV_LORA) / s * t.reshape(N_HEADS, V_HEAD, 1)),
            "wo": bf(np.random.standard_normal((DIM, HV)) / np.sqrt(HV) / t)}


def reference(o_lat, w_uv, wo):
    ol = mxq(f64(o_lat), 3, "e4m3").transpose(0, 2, 1, 3)
    wv = mxq(f64(w_uv), 2, "e4m3").transpose(0, 2, 1)
    o = ol @ wv[None]
    o = o.transpose(0, 2, 1, 3).reshape(B, S, HV)
    return mxq(o, 2, "e4m3") @ mxq(f64(wo), 1, "e4m3").T

@@ -1,0 +1,251 @@
+from contextlib import ExitStack
+
+import concourse.masks as masks
+import concourse.mybir as mybir
+
+BF16 = mybir.dt.bfloat16
+F32 = mybir.dt.float32
+U32 = mybir.dt.uint32
+U8 = mybir.dt.uint8
+FP8X4 = mybir.dt.float8_e4m3fn_x4
+
+P = 128
+S = 512
+HEADS = 16
+LATENT = 512
+V_HEAD = 128
+HV = HEADS * V_HEAD
+DIM = 2048
+
+FLOPS = 2 * S * HEADS * V_HEAD * LATENT + 2 * S * HV * DIM
+
+K_PASS = 512
+PAIRS = K_PASS // 2
+PIECE_COLS = 4096
+PIECE_PASSES = PIECE_COLS // K_PASS
+BANK_PASSES = 2
+S_TILES = S // P
+K_GROUPS = HV // K_PASS
+N_CHUNK = 512
+
+W_PIECES = HEADS * V_HEAD * LATENT // (P * PIECE_COLS)
+X_PIECES = DIM * HV // (P * PIECE_COLS)
+RAW_BUFS = 8
+
+
+def tile_mla_pc_kernel(tc, o_lat, w_uv, wo, out):
+    nc = tc.nc
+    with ExitStack() as ctx:
+        ctx.enter_context(tc.manual_schedule())
+        keep = ctx.enter_context(tc.tile_pool(name="keep", bufs=1))
+        raw_pool = ctx.enter_context(tc.tile_pool(name="raw", bufs=RAW_BUFS))
+        grouped_pool = ctx.enter_context(tc.tile_pool(name="grouped", bufs=3))
+        ol_pool = ctx.enter_context(tc.tile_pool(name="ol", bufs=3))
+        o_pool = ctx.enter_context(tc.tile_pool(name="o", bufs=3))
+        og_pool = ctx.enter_context(tc.tile_pool(name="og", bufs=3))
+        x_pool = ctx.enter_context(tc.tile_pool(name="x", bufs=2))
+        out_pool = ctx.enter_context(tc.tile_pool(name="outs", bufs=6))
+        flip_psum = ctx.enter_context(tc.psum_pool(name="flip", bufs=5))
+        acc_psum = ctx.enter_context(tc.psum_pool(name="acc", bufs=3))
+
+        ident = keep.tile([P, P], F32)
+        masks.make_identity(nc, ident[:])
+
+        w_codes = keep.tile([P, HEADS, V_HEAD], U32, align_bytes=64)
+        w_scales = keep.tile([P, HEADS, V_HEAD], U8, align_bytes=64)
+
+        o_codes = keep.tile([P, S_TILES, K_GROUPS, P], U32, align_bytes=64)
+        o_scales = keep.tile([P, S_TILES, K_GROUPS, P], U8, align_bytes=64)
+
+        pieces = []
+        for half in range(W_PIECES):
+            pieces.append(("w_uv", half))
+            pieces.extend([("o_lat", (tok, half)) for tok in range(S_TILES)])
+        pieces.extend([("wo", i) for i in range(X_PIECES)])
+        raw_of = {}
+        grouped_of = {}
+        ol_of = {}
+        o_of = {}
+        og_of = {}
+        x_of = {}
+
+        def load(j):
+            kind, i = pieces[j]
+            raw = raw_pool.tile([P, PIECE_COLS], BF16)
+            if kind == "w_uv":
+                nc.sync.dma_start(
+                    out=raw[:].rearrange("d (h c) -> d h c", c=LATENT),
+                    in_=w_uv[8 * i : 8 * i + 8, :, :].rearrange("h d c -> d h c"),
+                )
+            elif kind == "o_lat":
+                tok, half = i
+                nc.sync.dma_start(
+                    out=raw[:],
+                    in_=o_lat[0, tok * P : (tok + 1) * P, 8 * half : 8 * half + 8, :].rearrange(
+                        "s h c -> s (h c)"
+                    ),
+                )
+            else:
+                nc.sync.dma_start(
+                    out=raw[:].rearrange("p (j k) -> p j k", j=2),
+                    in_=wo[2 * i * P : (2 * i + 2) * P, :].rearrange("(j p) k -> p j k", p=P),
+                )
+            raw_of[j] = raw
+
+        def flip(j):
+            kind = pieces[j][0]
+            pairs = raw_of[j][:].bitcast(F32)
+            grouped = grouped_pool.tile([P, PIECE_COLS], BF16, align_bytes=64)
+            grouped_pairs = grouped[:].bitcast(F32).rearrange(
+                "p (a r u) -> p a r u", a=PIECE_PASSES, u=2
+            )
+            for b in range(PIECE_PASSES // BANK_PASSES):
+                bank = flip_psum.tile([P, BANK_PASSES, 2, P], F32)
+                for a in range(BANK_PASSES):
+                    if kind == "wo":
+                        first = a * (HV // 2) + b * PAIRS
+                    else:
+                        first = (b * BANK_PASSES + a) * PAIRS
+                    for u in range(2):
+                        nc.tensor.transpose(
+                            bank[:, a, u, :],
+                            pairs[:, first + u : first + PAIRS : 2],
+                            ident[:],
+                        )
+                src = bank[:].rearrange("p a u r -> p a r u")
+                dst = grouped_pairs[:, b * BANK_PASSES : (b + 1) * BANK_PASSES, :, :]
+                if b == 0:
+                    nc.vector.tensor_copy(out=dst, in_=src)
+                else:
+                    nc.scalar.copy(out=dst, in_=src)
+            grouped_of[j] = grouped
+
+        def quantise(j):
+            kind, i = pieces[j]
+            grouped = grouped_of[j]
+            if kind == "w_uv":
+                for gg in range(2):
+                    heads = slice(8 * i + 4 * gg, 8 * i + 4 * gg + 4)
+                    nc.vector.quantize_mx(
+                        out=w_codes[:, heads, :].rearrange("p h d -> p (h d)").bitcast(FP8X4),
+                        scales=w_scales[:, heads, :].rearrange("p h d -> p (h d)"),
+                        in_=grouped[:, gg * PIECE_COLS // 2 : (gg + 1) * PIECE_COLS // 2],
+                    )
+            elif kind == "o_lat":
+                ol_codes = ol_pool.tile([P, PIECE_PASSES, P], U32, align_bytes=64)
+                ol_scales = ol_pool.tile([P, PIECE_PASSES, P], U8, align_bytes=64)
+                for gg in range(2):
+                    heads = slice(4 * gg, 4 * gg + 4)
+                    nc.vector.quantize_mx(
+                        out=ol_codes[:, heads, :].rearrange("p h s -> p (h s)").bitcast(FP8X4),
+                        scales=ol_scales[:, heads, :].rearrange("p h s -> p (h s)"),
+                        in_=grouped[:, gg * PIECE_COLS // 2 : (gg + 1) * PIECE_COLS // 2],
+                    )
+                ol_of[j] = (ol_codes, ol_scales)
+            else:
+                chunk, part = divmod(i, 2)
+                if part == 0:
+                    x_codes = x_pool.tile([P, K_GROUPS, N_CHUNK], U32, align_bytes=64)
+                    x_scales = x_pool.tile([P, K_GROUPS, N_CHUNK], U8, align_bytes=64)
+                    x_of[chunk] = (x_codes, x_scales)
+                x_codes, x_scales = x_of[chunk]
+                cols = slice(part * 2 * P, (part + 1) * 2 * P)
+                for g in range(K_GROUPS):
+                    nc.vector.quantize_mx(
+                        out=x_codes[:, g, cols].bitcast(FP8X4),
+                        scales=x_scales[:, g, cols],
+                        in_=grouped[:, g * 8 * P : (g + 1) * 8 * P],
+                    )
+
+        def up_project(j):
+            tok, half = pieces[j][1]
+            ol_codes, ol_scales = ol_of[j]
+            o_rows = o_pool.tile([P, 2 * K_PASS], BF16, align_bytes=64)
+            for gg in range(2):
+                o_bank = acc_psum.tile([P, 4, P], F32, tag="acc")
+                for hh in range(4):
+                    head = 4 * gg + hh
+                    nc.tensor.matmul_mx(
+                        out=o_bank[:, hh, :],
+                        lhsT=ol_codes[:, head, :].bitcast(FP8X4),
+                        lhsT_scale=ol_scales[:, head, :],
+                        rhs=w_codes[:, 8 * half + head, :].bitcast(FP8X4),
+                        rhs_scale=w_scales[:, 8 * half + head, :],
+                        start=True,
+                        stop=True,
+                    )
+                nc.scalar.copy(
+                    out=o_rows[:, gg * K_PASS : (gg + 1) * K_PASS],
+                    in_=o_bank[:].rearrange("p h d -> p (h d)"),
+                )
+            o_of[j] = o_rows
+
+        def flip_o(j):
+            pairs = o_of[j][:].bitcast(F32)
+            o_grouped = og_pool.tile([P, 2, P, 4], BF16, align_bytes=64)
+            bank = flip_psum.tile([P, BANK_PASSES, 2, P], F32)
+            for gg in range(2):
+                for u in range(2):
+                    nc.tensor.transpose(
+                        bank[:, gg, u, :],
+                        pairs[:, gg * PAIRS + u : (gg + 1) * PAIRS : 2],
+                        ident[:],
+                    )
+            nc.scalar.copy(
+                out=o_grouped[:].rearrange("p g s t -> p (g s t)").bitcast(F32).rearrange(
+                    "p (g s u) -> p g s u", g=2, u=2
+                ),
+                in_=bank[:].rearrange("p g u s -> p g s u"),
+            )
+            og_of[j] = o_grouped
+
+        def quantise_o(j):
+            tok, half = pieces[j][1]
+            groups = slice(2 * half, 2 * half + 2)
+            nc.vector.quantize_mx(
+                out=o_codes[:, tok, groups, :].rearrange("p g s -> p (g s)").bitcast(FP8X4),
+                scales=o_scales[:, tok, groups, :].rearrange("p g s -> p (g s)"),
+                in_=og_of[j][:].rearrange("p g s t -> p (g s t)"),
+            )
+
+        def project_out(chunk):
+            x_codes, x_scales = x_of[chunk]
+            for tok in range(S_TILES):
+                out_bank = acc_psum.tile([P, N_CHUNK], F32, tag="acc")
+                for g in range(K_GROUPS):
+                    nc.tensor.matmul_mx(
+                        out=out_bank[:],
+                        lhsT=o_codes[:, tok, g, :].bitcast(FP8X4),
+                        lhsT_scale=o_scales[:, tok, g, :],
+                        rhs=x_codes[:, g, :].bitcast(FP8X4),
+                        rhs_scale=x_scales[:, g, :],
+                        start=(g == 0),
+                        stop=(g == K_GROUPS - 1),
+                    )
+                result = out_pool.tile([P, N_CHUNK], F32)
+                nc.scalar.copy(out=result[:], in_=out_bank[:])
+                nc.sync.dma_start(
+                    out=out[0, tok * P : (tok + 1) * P, chunk * N_CHUNK : (chunk + 1) * N_CHUNK],
+                    in_=result[:],
+                )
+
+        for j in range(RAW_BUFS):
+            load(j)
+        for j in range(len(pieces) + 2):
+            if j < len(pieces):
+                flip(j)
+            if 0 <= j - 3 < len(pieces) and pieces[j - 3][0] == "o_lat":
+                flip_o(j - 3)
+            if j < len(pieces):
+                if j + RAW_BUFS < len(pieces):
+                    load(j + RAW_BUFS)
+            if 0 <= j - 1 < len(pieces):
+                quantise(j - 1)
+            if 0 <= j - 4 < len(pieces) and pieces[j - 4][0] == "o_lat":
+                quantise_o(j - 4)
+            if 0 <= j - 2 < len(pieces):
+                kind, i = pieces[j - 2]
+                if kind == "o_lat":
+                    up_project(j - 2)
+                if kind == "wo" and i % 2 == 1:
+                    project_out(i // 2)

@@ -39,6 +39,7 @@ def tile_mla_pc_kernel(tc, o_lat, w_uv, wo, out):
         ctx.enter_context(tc.manual_schedule())
         keep = ctx.enter_context(tc.tile_pool(name="keep", bufs=1))
         raw_pool = ctx.enter_context(tc.tile_pool(name="raw", bufs=RAW_BUFS))
+        sorted_pool = ctx.enter_context(tc.tile_pool(name="sorted", bufs=3))
         grouped_pool = ctx.enter_context(tc.tile_pool(name="grouped", bufs=3))
         ol_pool = ctx.enter_context(tc.tile_pool(name="ol", bufs=3))
         o_pool = ctx.enter_context(tc.tile_pool(name="o", bufs=3))
@@ -63,6 +64,7 @@ def tile_mla_pc_kernel(tc, o_lat, w_uv, wo, out):
             pieces.extend([("o_lat", (tok, half)) for tok in range(S_TILES)])
         pieces.extend([("wo", i) for i in range(X_PIECES)])
         raw_of = {}
+        sorted_of = {}
         grouped_of = {}
         ol_of = {}
         o_of = {}
@@ -92,9 +94,17 @@ def tile_mla_pc_kernel(tc, o_lat, w_uv, wo, out):
                 )
             raw_of[j] = raw
 
+        def sort_words(j):
+            words = sorted_pool.tile([P, PIECE_COLS // 2], F32)
+            nc.vector.tensor_copy(
+                out=words[:].rearrange("p (a u w) -> p a u w", u=2, w=P),
+                in_=raw_of[j][:].bitcast(F32).rearrange("p (a w u) -> p a u w", u=2, w=P),
+            )
+            sorted_of[j] = words
+
         def flip(j):
             kind = pieces[j][0]
-            pairs = raw_of[j][:].bitcast(F32)
+            pairs = sorted_of[j][:]
             grouped = grouped_pool.tile([P, PIECE_COLS], BF16, align_bytes=64)
             grouped_pairs = grouped[:].bitcast(F32).rearrange(
                 "p (a r u) -> p a r u", a=PIECE_PASSES, u=2
@@ -109,7 +119,7 @@ def tile_mla_pc_kernel(tc, o_lat, w_uv, wo, out):
                     for u in range(2):
                         nc.tensor.transpose(
                             bank[:, a, u, :],
-                            pairs[:, first + u : first + PAIRS : 2],
+                            pairs[:, first + u * P : first + (u + 1) * P],
                             ident[:],
                         )
                 src = bank[:].rearrange("p a u r -> p a r u")
@@ -175,8 +185,12 @@ def tile_mla_pc_kernel(tc, o_lat, w_uv, wo, out):
                         stop=True,
                     )
                 nc.scalar.copy(
-                    out=o_rows[:, gg * K_PASS : (gg + 1) * K_PASS],
-                    in_=o_bank[:].rearrange("p h d -> p (h d)"),
+                    out=o_rows[:, gg * K_PASS : (gg + 1) * K_PASS].rearrange(
+                        "p (u w e) -> p u w e", u=2, e=2
+                    ),
+                    in_=o_bank[:].rearrange("p h d -> p (h d)").rearrange(
+                        "p (w u e) -> p u w e", u=2, e=2
+                    ),
                 )
             o_of[j] = o_rows
 
@@ -188,7 +202,7 @@ def tile_mla_pc_kernel(tc, o_lat, w_uv, wo, out):
                 for u in range(2):
                     nc.tensor.transpose(
                         bank[:, gg, u, :],
-                        pairs[:, gg * PAIRS + u : (gg + 1) * PAIRS : 2],
+                        pairs[:, gg * PAIRS + u * P : gg * PAIRS + (u + 1) * P],
                         ident[:],
                     )
             nc.scalar.copy(
@@ -231,14 +245,16 @@ def tile_mla_pc_kernel(tc, o_lat, w_uv, wo, out):
 
         for j in range(RAW_BUFS):
             load(j)
+        sort_words(0)
         for j in range(len(pieces) + 2):
             if j < len(pieces):
                 flip(j)
             if 0 <= j - 3 < len(pieces) and pieces[j - 3][0] == "o_lat":
                 flip_o(j - 3)
-            if j < len(pieces):
-                if j + RAW_BUFS < len(pieces):
-                    load(j + RAW_BUFS)
+            if j + 1 < len(pieces):
+                sort_words(j + 1)
+            if j + RAW_BUFS < len(pieces):
+                load(j + RAW_BUFS)
             if 0 <= j - 1 < len(pieces):
                 quantise(j - 1)
             if 0 <= j - 4 < len(pieces) and pieces[j - 4][0] == "o_lat":

@@ -23,6 +23,7 @@ K_PASS = 512
 PAIRS = K_PASS // 2
 PIECE_COLS = 4096
 PIECE_PASSES = PIECE_COLS // K_PASS
+RUN = 16
 BANK_PASSES = 2
 S_TILES = S // P
 K_GROUPS = HV // K_PASS
@@ -95,16 +96,16 @@ def tile_mla_pc_kernel(tc, o_lat, w_uv, wo, out):
             raw_of[j] = raw
 
         def sort_words(j):
-            words = sorted_pool.tile([P, PIECE_COLS // 2], F32)
+            words = sorted_pool.tile([P, PIECE_COLS], BF16)
             nc.vector.tensor_copy(
-                out=words[:].rearrange("p (a u w) -> p a u w", u=2, w=P),
-                in_=raw_of[j][:].bitcast(F32).rearrange("p (a w u) -> p a u w", u=2, w=P),
+                out=words[:].rearrange("p (u q e) -> p u q e", u=2, e=RUN),
+                in_=raw_of[j][:].rearrange("p (q u e) -> p u q e", u=2, e=RUN),
             )
             sorted_of[j] = words
 
         def flip(j):
             kind = pieces[j][0]
-            pairs = sorted_of[j][:]
+            pairs = sorted_of[j][:].bitcast(F32)
             grouped = grouped_pool.tile([P, PIECE_COLS], BF16, align_bytes=64)
             grouped_pairs = grouped[:].bitcast(F32).rearrange(
                 "p (a r u) -> p a r u", a=PIECE_PASSES, u=2
@@ -113,13 +114,14 @@ def tile_mla_pc_kernel(tc, o_lat, w_uv, wo, out):
                 bank = flip_psum.tile([P, BANK_PASSES, 2, P], F32)
                 for a in range(BANK_PASSES):
                     if kind == "wo":
-                        first = a * (HV // 2) + b * PAIRS
+                        operand = a * K_GROUPS + b
                     else:
-                        first = (b * BANK_PASSES + a) * PAIRS
+                        operand = b * BANK_PASSES + a
                     for u in range(2):
+                        first = u * (PIECE_COLS // 4) + operand * P
                         nc.tensor.transpose(
                             bank[:, a, u, :],
-                            pairs[:, first + u * P : first + (u + 1) * P],
+                            pairs[:, first : first + P],
                             ident[:],
                         )
                 src = bank[:].rearrange("p a u r -> p a r u")
@@ -186,10 +188,10 @@ def tile_mla_pc_kernel(tc, o_lat, w_uv, wo, out):
                     )
                 nc.scalar.copy(
                     out=o_rows[:, gg * K_PASS : (gg + 1) * K_PASS].rearrange(
-                        "p (u w e) -> p u w e", u=2, e=2
+                        "p (u q e) -> p u q e", u=2, e=RUN
                     ),
                     in_=o_bank[:].rearrange("p h d -> p (h d)").rearrange(
-                        "p (w u e) -> p u w e", u=2, e=2
+                        "p (q u e) -> p u q e", u=2, e=RUN
                     ),
                 )
             o_of[j] = o_rows

@@ -96,16 +96,16 @@ def tile_mla_pc_kernel(tc, o_lat, w_uv, wo, out):
             raw_of[j] = raw
 
         def sort_words(j):
-            words = sorted_pool.tile([P, PIECE_COLS], BF16)
-            nc.vector.tensor_copy(
-                out=words[:].rearrange("p (u q e) -> p u q e", u=2, e=RUN),
-                in_=raw_of[j][:].rearrange("p (q u e) -> p u q e", u=2, e=RUN),
-            )
+            words = sorted_pool.tile([P, 2, PIECE_COLS // 2], BF16)
+            runs = raw_of[j][:].rearrange("p (q u e) -> p u q e", u=2, e=RUN)
+            for u in range(2):
+                nc.vector.tensor_copy(
+                    out=words[:, u, :].rearrange("p (q e) -> p q e", e=RUN), in_=runs[:, u, :, :]
+                )
             sorted_of[j] = words
 
         def flip(j):
             kind = pieces[j][0]
-            pairs = sorted_of[j][:].bitcast(F32)
             grouped = grouped_pool.tile([P, PIECE_COLS], BF16, align_bytes=64)
             grouped_pairs = grouped[:].bitcast(F32).rearrange(
                 "p (a r u) -> p a r u", a=PIECE_PASSES, u=2
@@ -118,12 +118,13 @@ def tile_mla_pc_kernel(tc, o_lat, w_uv, wo, out):
                     else:
                         operand = b * BANK_PASSES + a
                     for u in range(2):
-                        first = u * (PIECE_COLS // 4) + operand * P
-                        nc.tensor.transpose(
-                            bank[:, a, u, :],
-                            pairs[:, first : first + P],
-                            ident[:],
-                        )
+                        if kind == "wo":
+                            pairs = sorted_of[j][:, u, :].bitcast(F32)
+                            words = pairs[:, operand * P : (operand + 1) * P]
+                        else:
+                            pairs = raw_of[j][:].bitcast(F32)
+                            words = pairs[:, operand * PAIRS + u : (operand + 1) * PAIRS : 2]
+                        nc.tensor.transpose(bank[:, a, u, :], words, ident[:])
                 src = bank[:].rearrange("p a u r -> p a r u")
                 dst = grouped_pairs[:, b * BANK_PASSES : (b + 1) * BANK_PASSES, :, :]
                 if b == 0:
@@ -247,13 +248,12 @@ def tile_mla_pc_kernel(tc, o_lat, w_uv, wo, out):
 
         for j in range(RAW_BUFS):
             load(j)
-        sort_words(0)
         for j in range(len(pieces) + 2):
             if j < len(pieces):
                 flip(j)
             if 0 <= j - 3 < len(pieces) and pieces[j - 3][0] == "o_lat":
                 flip_o(j - 3)
-            if j + 1 < len(pieces):
+            if j + 1 < len(pieces) and pieces[j + 1][0] == "wo":
                 sort_words(j + 1)
             if j + RAW_BUFS < len(pieces):
                 load(j + RAW_BUFS)

@@ -28,9 +28,9 @@ BANK_PASSES = 2
 S_TILES = S // P
 K_GROUPS = HV // K_PASS
 N_CHUNK = 512
+X_PIECES = 8
+X_COLS = 256
 
-W_PIECES = HEADS * V_HEAD * LATENT // (P * PIECE_COLS)
-X_PIECES = DIM * HV // (P * PIECE_COLS)
 RAW_BUFS = 8
 
 
@@ -45,7 +45,6 @@ def tile_mla_pc_kernel(tc, o_lat, w_uv, wo, out):
         ol_pool = ctx.enter_context(tc.tile_pool(name="ol", bufs=3))
         o_pool = ctx.enter_context(tc.tile_pool(name="o", bufs=3))
         og_pool = ctx.enter_context(tc.tile_pool(name="og", bufs=3))
-        x_pool = ctx.enter_context(tc.tile_pool(name="x", bufs=2))
         out_pool = ctx.enter_context(tc.tile_pool(name="outs", bufs=6))
         flip_psum = ctx.enter_context(tc.psum_pool(name="flip", bufs=5))
         acc_psum = ctx.enter_context(tc.psum_pool(name="acc", bufs=3))
@@ -55,31 +54,35 @@ def tile_mla_pc_kernel(tc, o_lat, w_uv, wo, out):
 
         w_codes = keep.tile([P, HEADS, V_HEAD], U32, align_bytes=64)
         w_scales = keep.tile([P, HEADS, V_HEAD], U8, align_bytes=64)
-
         o_codes = keep.tile([P, S_TILES, K_GROUPS, P], U32, align_bytes=64)
         o_scales = keep.tile([P, S_TILES, K_GROUPS, P], U8, align_bytes=64)
+        x_codes = keep.tile([P, X_PIECES, K_GROUPS, X_COLS], U32, align_bytes=64)
+        x_scales = keep.tile([P, X_PIECES, K_GROUPS, X_COLS], U8, align_bytes=64)
 
-        pieces = []
-        for half in range(W_PIECES):
-            pieces.append(("w_uv", half))
-            pieces.extend([("o_lat", (tok, half)) for tok in range(S_TILES)])
-        pieces.extend([("wo", i) for i in range(X_PIECES)])
+        pieces = [("w_uv", 0), ("w_uv", 1)]
+        pieces.extend([("o_lat", (tok, half)) for tok in range(2) for half in range(2)])
+        pieces.extend([("wo", 0), ("wo", 1), ("o_lat", (2, 0)), ("o_lat", (2, 1))])
+        pieces.extend([("wo", 2), ("wo", 3), ("o_lat", (3, 0)), ("o_lat", (3, 1))])
+        pieces.extend([("wo", i) for i in range(4, X_PIECES)])
+        count = len(pieces)
         raw_of = {}
         sorted_of = {}
         grouped_of = {}
         ol_of = {}
         o_of = {}
         og_of = {}
-        x_of = {}
 
         def load(j):
             kind, i = pieces[j]
             raw = raw_pool.tile([P, PIECE_COLS], BF16)
             if kind == "w_uv":
-                nc.sync.dma_start(
-                    out=raw[:].rearrange("d (h c) -> d h c", c=LATENT),
-                    in_=w_uv[8 * i : 8 * i + 8, :, :].rearrange("h d c -> d h c"),
-                )
+                n = 4 if j == 0 else 1
+                for q in range(n):
+                    w = 8 // n
+                    nc.sync.dma_start(
+                        out=raw[:, q * w * LATENT : (q + 1) * w * LATENT].rearrange("d (h c) -> d h c", c=LATENT),
+                        in_=w_uv[8 * i + q * w : 8 * i + (q + 1) * w, :, :].rearrange("h d c -> d h c"),
+                    )
             elif kind == "o_lat":
                 tok, half = i
                 nc.sync.dma_start(
@@ -95,13 +98,17 @@ def tile_mla_pc_kernel(tc, o_lat, w_uv, wo, out):
                 )
             raw_of[j] = raw
 
+        def is_sorted(j):
+            return pieces[j][0] == "wo"
+
         def sort_words(j):
-            words = sorted_pool.tile([P, 2, PIECE_COLS // 2], BF16)
-            runs = raw_of[j][:].rearrange("p (q u e) -> p u q e", u=2, e=RUN)
-            for u in range(2):
-                nc.vector.tensor_copy(
-                    out=words[:, u, :].rearrange("p (q e) -> p q e", e=RUN), in_=runs[:, u, :, :]
-                )
+            if not is_sorted(j):
+                return
+            words = sorted_pool.tile([P, PIECE_COLS], BF16)
+            nc.vector.tensor_copy(
+                out=words[:].rearrange("p (u q e) -> p u q e", u=2, e=RUN),
+                in_=raw_of[j][:].rearrange("p (q u e) -> p u q e", u=2, e=RUN),
+            )
             sorted_of[j] = words
 
         def flip(j):
@@ -118,16 +125,16 @@ def tile_mla_pc_kernel(tc, o_lat, w_uv, wo, out):
                     else:
                         operand = b * BANK_PASSES + a
                     for u in range(2):
-                        if kind == "wo":
-                            pairs = sorted_of[j][:, u, :].bitcast(F32)
-                            words = pairs[:, operand * P : (operand + 1) * P]
+                        if is_sorted(j):
+                            first = (u * PIECE_PASSES + operand) * P
+                            src = sorted_of[j][:].bitcast(F32)[:, first : first + P]
                         else:
-                            pairs = raw_of[j][:].bitcast(F32)
-                            words = pairs[:, operand * PAIRS + u : (operand + 1) * PAIRS : 2]
-                        nc.tensor.transpose(bank[:, a, u, :], words, ident[:])
+                            first = operand * PAIRS
+                            src = raw_of[j][:].bitcast(F32)[:, first + u : first + PAIRS : 2]
+                        nc.tensor.transpose(bank[:, a, u, :], src, ident[:])
                 src = bank[:].rearrange("p a u r -> p a r u")
                 dst = grouped_pairs[:, b * BANK_PASSES : (b + 1) * BANK_PASSES, :, :]
-                if b == 0:
+                if b == 0 or (b == 2 and kind == "w_uv"):
                     nc.vector.tensor_copy(out=dst, in_=src)
                 else:
                     nc.scalar.copy(out=dst, in_=src)
@@ -156,17 +163,10 @@ def tile_mla_pc_kernel(tc, o_lat, w_uv, wo, out):
                     )
                 ol_of[j] = (ol_codes, ol_scales)
             else:
-                chunk, part = divmod(i, 2)
-                if part == 0:
-                    x_codes = x_pool.tile([P, K_GROUPS, N_CHUNK], U32, align_bytes=64)
-                    x_scales = x_pool.tile([P, K_GROUPS, N_CHUNK], U8, align_bytes=64)
-                    x_of[chunk] = (x_codes, x_scales)
-                x_codes, x_scales = x_of[chunk]
-                cols = slice(part * 2 * P, (part + 1) * 2 * P)
                 for g in range(K_GROUPS):
                     nc.vector.quantize_mx(
-                        out=x_codes[:, g, cols].bitcast(FP8X4),
-                        scales=x_scales[:, g, cols],
+                        out=x_codes[:, i, g, :].bitcast(FP8X4),
+                        scales=x_scales[:, i, g, :],
                         in_=grouped[:, g * 8 * P : (g + 1) * 8 * P],
                     )
 
@@ -203,11 +203,8 @@ def tile_mla_pc_kernel(tc, o_lat, w_uv, wo, out):
             bank = flip_psum.tile([P, BANK_PASSES, 2, P], F32)
             for gg in range(2):
                 for u in range(2):
-                    nc.tensor.transpose(
-                        bank[:, gg, u, :],
-                        pairs[:, gg * PAIRS + u * P : gg * PAIRS + (u + 1) * P],
-                        ident[:],
-                    )
+                    first = (2 * gg + u) * P
+                    nc.tensor.transpose(bank[:, gg, u, :], pairs[:, first : first + P], ident[:])
             nc.scalar.copy(
                 out=o_grouped[:].rearrange("p g s t -> p (g s t)").bitcast(F32).rearrange(
                     "p (g s u) -> p g s u", g=2, u=2
@@ -225,45 +222,66 @@ def tile_mla_pc_kernel(tc, o_lat, w_uv, wo, out):
                 in_=og_of[j][:].rearrange("p g s t -> p (g s t)"),
             )
 
-        def project_out(chunk):
-            x_codes, x_scales = x_of[chunk]
-            for tok in range(S_TILES):
-                out_bank = acc_psum.tile([P, N_CHUNK], F32, tag="acc")
+        def project_out(step, blocks):
+            out_bank = acc_psum.tile([P, 2, X_COLS], F32, tag="acc")
+            result = out_pool.tile([P, 2, X_COLS], F32)
+            n = len(blocks)
+            for b in range(n):
+                tok, i = blocks[b]
                 for g in range(K_GROUPS):
                     nc.tensor.matmul_mx(
-                        out=out_bank[:],
+                        out=out_bank[:, b, :],
                         lhsT=o_codes[:, tok, g, :].bitcast(FP8X4),
                         lhsT_scale=o_scales[:, tok, g, :],
-                        rhs=x_codes[:, g, :].bitcast(FP8X4),
-                        rhs_scale=x_scales[:, g, :],
+                        rhs=x_codes[:, i, g, :].bitcast(FP8X4),
+                        rhs_scale=x_scales[:, i, g, :],
                         start=(g == 0),
                         stop=(g == K_GROUPS - 1),
                     )
-                result = out_pool.tile([P, N_CHUNK], F32)
-                nc.scalar.copy(out=result[:], in_=out_bank[:])
+            if step >= count and step % 2 == 0:
+                nc.vector.tensor_copy(out=result[:, 0:n, :], in_=out_bank[:, 0:n, :])
+            else:
+                nc.scalar.copy(out=result[:, 0:n, :], in_=out_bank[:, 0:n, :])
+            for b in range(n):
+                tok, i = blocks[b]
                 nc.sync.dma_start(
-                    out=out[0, tok * P : (tok + 1) * P, chunk * N_CHUNK : (chunk + 1) * N_CHUNK],
-                    in_=result[:],
+                    out=out[0, tok * P : (tok + 1) * P, i * X_COLS : (i + 1) * X_COLS],
+                    in_=result[:, b, :],
                 )
 
         for j in range(RAW_BUFS):
             load(j)
-        for j in range(len(pieces) + 2):
-            if j < len(pieces):
-                flip(j)
-            if 0 <= j - 3 < len(pieces) and pieces[j - 3][0] == "o_lat":
-                flip_o(j - 3)
-            if j + 1 < len(pieces) and pieces[j + 1][0] == "wo":
-                sort_words(j + 1)
-            if j + RAW_BUFS < len(pieces):
-                load(j + RAW_BUFS)
-            if 0 <= j - 1 < len(pieces):
-                quantise(j - 1)
-            if 0 <= j - 4 < len(pieces) and pieces[j - 4][0] == "o_lat":
-                quantise_o(j - 4)
-            if 0 <= j - 2 < len(pieces):
-                kind, i = pieces[j - 2]
-                if kind == "o_lat":
-                    up_project(j - 2)
-                if kind == "wo" and i % 2 == 1:
-                    project_out(i // 2)
+        toks = []
+        chunks = []
+        waiting = []
+        step = -2
+        while step < count + 5 or waiting:
+            j = step - 1
+            if 0 <= j < count:
+                quantise(j)
+                if pieces[j][0] == "wo":
+                    chunks.append(pieces[j][1])
+                    waiting.extend([(tok, pieces[j][1]) for tok in toks])
+            if 0 <= step < count:
+                flip(step)
+                if step + RAW_BUFS < count:
+                    load(step + RAW_BUFS)
+            if 0 <= step - 3 < count and pieces[step - 3][0] == "o_lat":
+                flip_o(step - 3)
+            if step + 2 < count:
+                sort_words(step + 2)
+            if 0 <= step - 2 < count and pieces[step - 2][0] == "o_lat":
+                up_project(step - 2)
+            for pair in range(2):
+                blocks = waiting[:2]
+                if blocks:
+                    project_out(step, blocks)
+                    for block in blocks:
+                        waiting.remove(block)
+            if 0 <= step - 4 < count and pieces[step - 4][0] == "o_lat":
+                quantise_o(step - 4)
+                tok, half = pieces[step - 4][1]
+                if half == 1:
+                    toks.append(tok)
+                    waiting.extend([(tok, i) for i in chunks])
+            step += 1

@@ -106,8 +106,8 @@ def tile_mla_pc_kernel(tc, o_lat, w_uv, wo, out):
                 return
             words = sorted_pool.tile([P, PIECE_COLS], BF16)
             nc.vector.tensor_copy(
-                out=words[:].rearrange("p (u q e) -> p u q e", u=2, e=RUN),
-                in_=raw_of[j][:].rearrange("p (q u e) -> p u q e", u=2, e=RUN),
+                out=words[:].rearrange("p (u q e) -> p q u e", u=2, e=RUN),
+                in_=raw_of[j][:].rearrange("p (q u e) -> p q u e", u=2, e=RUN),
             )
             sorted_of[j] = words
 
@@ -189,10 +189,10 @@ def tile_mla_pc_kernel(tc, o_lat, w_uv, wo, out):
                     )
                 nc.scalar.copy(
                     out=o_rows[:, gg * K_PASS : (gg + 1) * K_PASS].rearrange(
-                        "p (u q e) -> p u q e", u=2, e=RUN
+                        "p (u q e) -> p q u e", u=2, e=RUN
                     ),
                     in_=o_bank[:].rearrange("p h d -> p (h d)").rearrange(
-                        "p (q u e) -> p u q e", u=2, e=RUN
+                        "p (q u e) -> p q u e", u=2, e=RUN
                     ),
                 )
             o_of[j] = o_rows

@@ -60,10 +60,8 @@ def tile_mla_pc_kernel(tc, o_lat, w_uv, wo, out):
         x_scales = keep.tile([P, X_PIECES, K_GROUPS, X_COLS], U8, align_bytes=64)
 
         pieces = [("w_uv", 0), ("w_uv", 1)]
-        pieces.extend([("o_lat", (tok, half)) for tok in range(2) for half in range(2)])
-        pieces.extend([("wo", 0), ("wo", 1), ("o_lat", (2, 0)), ("o_lat", (2, 1))])
-        pieces.extend([("wo", 2), ("wo", 3), ("o_lat", (3, 0)), ("o_lat", (3, 1))])
-        pieces.extend([("wo", i) for i in range(4, X_PIECES)])
+        pieces.extend([("o_lat", (tok, half)) for tok in range(S_TILES) for half in range(2)])
+        pieces.extend([("wo", i) for i in range(X_PIECES)])
         count = len(pieces)
         raw_of = {}
         sorted_of = {}
@@ -254,7 +252,7 @@ def tile_mla_pc_kernel(tc, o_lat, w_uv, wo, out):
         toks = []
         chunks = []
         waiting = []
-        step = -2
+        step = 0
         while step < count + 5 or waiting:
             j = step - 1
             if 0 <= j < count:
@@ -266,10 +264,6 @@ def tile_mla_pc_kernel(tc, o_lat, w_uv, wo, out):
                 flip(step)
                 if step + RAW_BUFS < count:
                     load(step + RAW_BUFS)
-            if 0 <= step - 3 < count and pieces[step - 3][0] == "o_lat":
-                flip_o(step - 3)
-            if step + 2 < count:
-                sort_words(step + 2)
             if 0 <= step - 2 < count and pieces[step - 2][0] == "o_lat":
                 up_project(step - 2)
             for pair in range(2):
@@ -278,6 +272,10 @@ def tile_mla_pc_kernel(tc, o_lat, w_uv, wo, out):
                     project_out(step, blocks)
                     for block in blocks:
                         waiting.remove(block)
+            if 0 <= step - 3 < count and pieces[step - 3][0] == "o_lat":
+                flip_o(step - 3)
+            if 0 <= step + 1 < count:
+                sort_words(step + 1)
             if 0 <= step - 4 < count and pieces[step - 4][0] == "o_lat":
                 quantise_o(step - 4)
                 tok, half = pieces[step - 4][1]

@@ -30,6 +30,7 @@ K_GROUPS = HV // K_PASS
 N_CHUNK = 512
 X_PIECES = 8
 X_COLS = 256
+UNSORTED = 4
 
 RAW_BUFS = 8
 
@@ -51,6 +52,9 @@ def tile_mla_pc_kernel(tc, o_lat, w_uv, wo, out):
 
         ident = keep.tile([P, P], F32)
         masks.make_identity(nc, ident[:])
+
+        warm = keep.tile([P, N_CHUNK], BF16)
+        nc.gpsimd.memset(warm[:], 0)
 
         w_codes = keep.tile([P, HEADS, V_HEAD], U32, align_bytes=64)
         w_scales = keep.tile([P, HEADS, V_HEAD], U8, align_bytes=64)
@@ -96,16 +100,15 @@ def tile_mla_pc_kernel(tc, o_lat, w_uv, wo, out):
                 )
             raw_of[j] = raw
 
-        def is_sorted(j):
-            return pieces[j][0] == "wo"
+        def first_sorted(j):
+            return 0 if pieces[j][0] == "wo" else UNSORTED
 
         def sort_words(j):
-            if not is_sorted(j):
-                return
+            start = first_sorted(j) * K_PASS
             words = sorted_pool.tile([P, PIECE_COLS], BF16)
             nc.vector.tensor_copy(
-                out=words[:].rearrange("p (u q e) -> p q u e", u=2, e=RUN),
-                in_=raw_of[j][:].rearrange("p (q u e) -> p q u e", u=2, e=RUN),
+                out=words[:, start:].rearrange("p (u q e) -> p q u e", u=2, e=RUN),
+                in_=raw_of[j][:, start:].rearrange("p (q u e) -> p q u e", u=2, e=RUN),
             )
             sorted_of[j] = words
 
@@ -117,14 +120,23 @@ def tile_mla_pc_kernel(tc, o_lat, w_uv, wo, out):
             )
             for b in range(PIECE_PASSES // BANK_PASSES):
                 bank = flip_psum.tile([P, BANK_PASSES, 2, P], F32)
+                if kind != "wo" and b % 2 == 0:
+                    nc.tensor.matmul(
+                        out=bank[:].rearrange("p a u r -> p (a u r)"),
+                        lhsT=warm[:, 0:P],
+                        rhs=warm[:],
+                        start=True,
+                        stop=True,
+                    )
                 for a in range(BANK_PASSES):
                     if kind == "wo":
                         operand = a * K_GROUPS + b
                     else:
                         operand = b * BANK_PASSES + a
                     for u in range(2):
-                        if is_sorted(j):
-                            first = (u * PIECE_PASSES + operand) * P
+                        start = first_sorted(j)
+                        if operand >= start:
+                            first = (2 * start + u * (PIECE_PASSES - start) + operand - start) * P
                             src = sorted_of[j][:].bitcast(F32)[:, first : first + P]
                         else:
                             first = operand * PAIRS
@@ -249,6 +261,7 @@ def tile_mla_pc_kernel(tc, o_lat, w_uv, wo, out):
 
         for j in range(RAW_BUFS):
             load(j)
+        sort_words(0)
         toks = []
         chunks = []
         waiting = []

@@ -53,9 +53,6 @@ def tile_mla_pc_kernel(tc, o_lat, w_uv, wo, out):
         ident = keep.tile([P, P], F32)
         masks.make_identity(nc, ident[:])
 
-        warm = keep.tile([P, N_CHUNK], BF16)
-        nc.gpsimd.memset(warm[:], 0)
-
         w_codes = keep.tile([P, HEADS, V_HEAD], U32, align_bytes=64)
         w_scales = keep.tile([P, HEADS, V_HEAD], U8, align_bytes=64)
         o_codes = keep.tile([P, S_TILES, K_GROUPS, P], U32, align_bytes=64)
@@ -120,14 +117,6 @@ def tile_mla_pc_kernel(tc, o_lat, w_uv, wo, out):
             )
             for b in range(PIECE_PASSES // BANK_PASSES):
                 bank = flip_psum.tile([P, BANK_PASSES, 2, P], F32)
-                if kind != "wo" and b % 2 == 0:
-                    nc.tensor.matmul(
-                        out=bank[:].rearrange("p a u r -> p (a u r)"),
-                        lhsT=warm[:, 0:P],
-                        rhs=warm[:],
-                        start=True,
-                        stop=True,
-                    )
                 for a in range(BANK_PASSES):
                     if kind == "wo":
                         operand = a * K_GROUPS + b

@@ -53,15 +53,16 @@ def tile_mla_pc_kernel(tc, o_lat, w_uv, wo, out):
         ident = keep.tile([P, P], F32)
         masks.make_identity(nc, ident[:])
 
-        w_codes = keep.tile([P, HEADS, V_HEAD], U32, align_bytes=64)
-        w_scales = keep.tile([P, HEADS, V_HEAD], U8, align_bytes=64)
-        o_codes = keep.tile([P, S_TILES, K_GROUPS, P], U32, align_bytes=64)
-        o_scales = keep.tile([P, S_TILES, K_GROUPS, P], U8, align_bytes=64)
-        x_codes = keep.tile([P, X_PIECES, K_GROUPS, X_COLS], U32, align_bytes=64)
-        x_scales = keep.tile([P, X_PIECES, K_GROUPS, X_COLS], U8, align_bytes=64)
+        w_codes = keep.tile([P, HEADS, V_HEAD], U32, align_bytes=256)
+        w_scales = keep.tile([P, HEADS, V_HEAD], U8, align_bytes=256)
+        o_codes = keep.tile([P, S_TILES, K_GROUPS, P], U32, align_bytes=256)
+        o_scales = keep.tile([P, S_TILES, K_GROUPS, P], U8, align_bytes=256)
+        x_codes = keep.tile([P, X_PIECES, K_GROUPS, X_COLS], U32, align_bytes=256)
+        x_scales = keep.tile([P, X_PIECES, K_GROUPS, X_COLS], U8, align_bytes=256)
 
-        pieces = [("w_uv", 0), ("w_uv", 1)]
-        pieces.extend([("o_lat", (tok, half)) for tok in range(S_TILES) for half in range(2)])
+        pieces = [("w_uv", 0), ("o_lat", (0, 0)), ("o_lat", (1, 0))]
+        pieces.extend([("w_uv", 1), ("o_lat", (0, 1)), ("o_lat", (1, 1))])
+        pieces.extend([("o_lat", (tok, half)) for tok in range(2, S_TILES) for half in range(2)])
         pieces.extend([("wo", i) for i in range(X_PIECES)])
         count = len(pieces)
         raw_of = {}
@@ -133,7 +134,7 @@ def tile_mla_pc_kernel(tc, o_lat, w_uv, wo, out):
                         nc.tensor.transpose(bank[:, a, u, :], src, ident[:])
                 src = bank[:].rearrange("p a u r -> p a r u")
                 dst = grouped_pairs[:, b * BANK_PASSES : (b + 1) * BANK_PASSES, :, :]
-                if b == 0 or (b == 2 and kind == "w_uv"):
+                if b == 0:
                     nc.vector.tensor_copy(out=dst, in_=src)
                 else:
                     nc.scalar.copy(out=dst, in_=src)
@@ -221,7 +222,7 @@ def tile_mla_pc_kernel(tc, o_lat, w_uv, wo, out):
                 in_=og_of[j][:].rearrange("p g s t -> p (g s t)"),
             )
 
-        def project_out(step, blocks):
+        def project_out(blocks, on_vector):
             out_bank = acc_psum.tile([P, 2, X_COLS], F32, tag="acc")
             result = out_pool.tile([P, 2, X_COLS], F32)
             n = len(blocks)
@@ -237,7 +238,7 @@ def tile_mla_pc_kernel(tc, o_lat, w_uv, wo, out):
                         start=(g == 0),
                         stop=(g == K_GROUPS - 1),
                     )
-            if step >= count and step % 2 == 0:
+            if on_vector:
                 nc.vector.tensor_copy(out=result[:, 0:n, :], in_=out_bank[:, 0:n, :])
             else:
                 nc.scalar.copy(out=result[:, 0:n, :], in_=out_bank[:, 0:n, :])
@@ -266,16 +267,18 @@ def tile_mla_pc_kernel(tc, o_lat, w_uv, wo, out):
                 flip(step)
                 if step + RAW_BUFS < count:
                     load(step + RAW_BUFS)
-            if 0 <= step - 2 < count and pieces[step - 2][0] == "o_lat":
-                up_project(step - 2)
-            for pair in range(2):
-                blocks = waiting[:2]
-                if blocks:
-                    project_out(step, blocks)
-                    for block in blocks:
-                        waiting.remove(block)
             if 0 <= step - 3 < count and pieces[step - 3][0] == "o_lat":
                 flip_o(step - 3)
+            if 0 <= step - 2 < count and pieces[step - 2][0] == "o_lat":
+                up_project(step - 2)
+            pairs = [waiting[:2], waiting[2:4]]
+            if step >= count and len(waiting) <= 4:
+                pairs = [waiting[:2], waiting[2:3], waiting[3:4]]
+            for n in range(len(pairs)):
+                if pairs[n]:
+                    project_out(pairs[n], step >= count and n % 2 == 1)
+                    for block in pairs[n]:
+                        waiting.remove(block)
             if 0 <= step + 1 < count:
                 sort_words(step + 1)
             if 0 <= step - 4 < count and pieces[step - 4][0] == "o_lat":

from contextlib import ExitStack

import concourse.masks as masks
import concourse.mybir as mybir

BF16 = mybir.dt.bfloat16
F32 = mybir.dt.float32
U32 = mybir.dt.uint32
U8 = mybir.dt.uint8
FP8X4 = mybir.dt.float8_e4m3fn_x4

P = 128
S = 512
HEADS = 16
LATENT = 512
V_HEAD = 128
HV = HEADS * V_HEAD
DIM = 2048

FLOPS = 2 * S * HEADS * V_HEAD * LATENT + 2 * S * HV * DIM

K_PASS = 512
PAIRS = K_PASS // 2
PIECE_COLS = 4096
PIECE_PASSES = PIECE_COLS // K_PASS
RUN = 16
BANK_PASSES = 2
S_TILES = S // P
K_GROUPS = HV // K_PASS
N_CHUNK = 512
X_PIECES = 8
X_COLS = 256
UNSORTED = 4

RAW_BUFS = 8


def tile_mla_pc_kernel(tc, o_lat, w_uv, wo, out):
    nc = tc.nc
    with ExitStack() as ctx:
        ctx.enter_context(tc.manual_schedule())
        keep = ctx.enter_context(tc.tile_pool(name="keep", bufs=1))
        raw_pool = ctx.enter_context(tc.tile_pool(name="raw", bufs=RAW_BUFS))
        sorted_pool = ctx.enter_context(tc.tile_pool(name="sorted", bufs=3))
        grouped_pool = ctx.enter_context(tc.tile_pool(name="grouped", bufs=3))
        ol_pool = ctx.enter_context(tc.tile_pool(name="ol", bufs=3))
        o_pool = ctx.enter_context(tc.tile_pool(name="o", bufs=3))
        og_pool = ctx.enter_context(tc.tile_pool(name="og", bufs=3))
        out_pool = ctx.enter_context(tc.tile_pool(name="outs", bufs=6))
        flip_psum = ctx.enter_context(tc.psum_pool(name="flip", bufs=5))
        acc_psum = ctx.enter_context(tc.psum_pool(name="acc", bufs=3))

        ident = keep.tile([P, P], F32)
        masks.make_identity(nc, ident[:])

        w_codes = keep.tile([P, HEADS, V_HEAD], U32, align_bytes=256)
        w_scales = keep.tile([P, HEADS, V_HEAD], U8, align_bytes=256)
        o_codes = keep.tile([P, S_TILES, K_GROUPS, P], U32, align_bytes=256)
        o_scales = keep.tile([P, S_TILES, K_GROUPS, P], U8, align_bytes=256)
        x_codes = keep.tile([P, X_PIECES, K_GROUPS, X_COLS], U32, align_bytes=256)
        x_scales = keep.tile([P, X_PIECES, K_GROUPS, X_COLS], U8, align_bytes=256)

        pieces = [("w_uv", 0), ("o_lat", (0, 0)), ("o_lat", (1, 0))]
        pieces.extend([("w_uv", 1), ("o_lat", (0, 1)), ("o_lat", (1, 1))])
        pieces.extend([("o_lat", (tok, half)) for tok in range(2, S_TILES) for half in range(2)])
        pieces.extend([("wo", i) for i in range(X_PIECES)])
        count = len(pieces)
        raw_of = {}
        sorted_of = {}
        grouped_of = {}
        ol_of = {}
        o_of = {}
        og_of = {}

        def load(j):
            kind, i = pieces[j]
            raw = raw_pool.tile([P, PIECE_COLS], BF16)
            if kind == "w_uv":
                n = 4 if j == 0 else 1
                for q in range(n):
                    w = 8 // n
                    nc.sync.dma_start(
                        out=raw[:, q * w * LATENT : (q + 1) * w * LATENT].rearrange("d (h c) -> d h c", c=LATENT),
                        in_=w_uv[8 * i + q * w : 8 * i + (q + 1) * w, :, :].rearrange("h d c -> d h c"),
                    )
            elif kind == "o_lat":
                tok, half = i
                nc.sync.dma_start(
                    out=raw[:],
                    in_=o_lat[0, tok * P : (tok + 1) * P, 8 * half : 8 * half + 8, :].rearrange(
                        "s h c -> s (h c)"
                    ),
                )
            else:
                nc.sync.dma_start(
                    out=raw[:].rearrange("p (j k) -> p j k", j=2),
                    in_=wo[2 * i * P : (2 * i + 2) * P, :].rearrange("(j p) k -> p j k", p=P),
                )
            raw_of[j] = raw

        def first_sorted(j):
            return 0 if pieces[j][0] == "wo" else UNSORTED

        def sort_words(j):
            start = first_sorted(j) * K_PASS
            words = sorted_pool.tile([P, PIECE_COLS], BF16)
            nc.vector.tensor_copy(
                out=words[:, start:].rearrange("p (u q e) -> p q u e", u=2, e=RUN),
                in_=raw_of[j][:, start:].rearrange("p (q u e) -> p q u e", u=2, e=RUN),
            )
            sorted_of[j] = words

        def flip(j):
            kind = pieces[j][0]
            grouped = grouped_pool.tile([P, PIECE_COLS], BF16, align_bytes=64)
            grouped_pairs = grouped[:].bitcast(F32).rearrange(
                "p (a r u) -> p a r u", a=PIECE_PASSES, u=2
            )
            for b in range(PIECE_PASSES // BANK_PASSES):
                bank = flip_psum.tile([P, BANK_PASSES, 2, P], F32)
                for a in range(BANK_PASSES):
                    if kind == "wo":
                        operand = a * K_GROUPS + b
                    else:
                        operand = b * BANK_PASSES + a
                    for u in range(2):
                        start = first_sorted(j)
                        if operand >= start:
                            first = (2 * start + u * (PIECE_PASSES - start) + operand - start) * P
                            src = sorted_of[j][:].bitcast(F32)[:, first : first + P]
                        else:
                            first = operand * PAIRS
                            src = raw_of[j][:].bitcast(F32)[:, first + u : first + PAIRS : 2]
                        nc.tensor.transpose(bank[:, a, u, :], src, ident[:])
                src = bank[:].rearrange("p a u r -> p a r u")
                dst = grouped_pairs[:, b * BANK_PASSES : (b + 1) * BANK_PASSES, :, :]
                if b == 0:
                    nc.vector.tensor_copy(out=dst, in_=src)
                else:
                    nc.scalar.copy(out=dst, in_=src)
            grouped_of[j] = grouped

        def quantise(j):
            kind, i = pieces[j]
            grouped = grouped_of[j]
            if kind == "w_uv":
                for gg in range(2):
                    heads = slice(8 * i + 4 * gg, 8 * i + 4 * gg + 4)
                    nc.vector.quantize_mx(
                        out=w_codes[:, heads, :].rearrange("p h d -> p (h d)").bitcast(FP8X4),
                        scales=w_scales[:, heads, :].rearrange("p h d -> p (h d)"),
                        in_=grouped[:, gg * PIECE_COLS // 2 : (gg + 1) * PIECE_COLS // 2],
                    )
            elif kind == "o_lat":
                ol_codes = ol_pool.tile([P, PIECE_PASSES, P], U32, align_bytes=64)
                ol_scales = ol_pool.tile([P, PIECE_PASSES, P], U8, align_bytes=64)
                for gg in range(2):
                    heads = slice(4 * gg, 4 * gg + 4)
                    nc.vector.quantize_mx(
                        out=ol_codes[:, heads, :].rearrange("p h s -> p (h s)").bitcast(FP8X4),
                        scales=ol_scales[:, heads, :].rearrange("p h s -> p (h s)"),
                        in_=grouped[:, gg * PIECE_COLS // 2 : (gg + 1) * PIECE_COLS // 2],
                    )
                ol_of[j] = (ol_codes, ol_scales)
            else:
                for g in range(K_GROUPS):
                    nc.vector.quantize_mx(
                        out=x_codes[:, i, g, :].bitcast(FP8X4),
                        scales=x_scales[:, i, g, :],
                        in_=grouped[:, g * 8 * P : (g + 1) * 8 * P],
                    )

        def up_project(j):
            tok, half = pieces[j][1]
            ol_codes, ol_scales = ol_of[j]
            o_rows = o_pool.tile([P, 2 * K_PASS], BF16, align_bytes=64)
            for gg in range(2):
                o_bank = acc_psum.tile([P, 4, P], F32, tag="acc")
                for hh in range(4):
                    head = 4 * gg + hh
                    nc.tensor.matmul_mx(
                        out=o_bank[:, hh, :],
                        lhsT=ol_codes[:, head, :].bitcast(FP8X4),
                        lhsT_scale=ol_scales[:, head, :],
                        rhs=w_codes[:, 8 * half + head, :].bitcast(FP8X4),
                        rhs_scale=w_scales[:, 8 * half + head, :],
                        start=True,
                        stop=True,
                    )
                nc.scalar.copy(
                    out=o_rows[:, gg * K_PASS : (gg + 1) * K_PASS].rearrange(
                        "p (u q e) -> p q u e", u=2, e=RUN
                    ),
                    in_=o_bank[:].rearrange("p h d -> p (h d)").rearrange(
                        "p (q u e) -> p q u e", u=2, e=RUN
                    ),
                )
            o_of[j] = o_rows

        def flip_o(j):
            pairs = o_of[j][:].bitcast(F32)
            o_grouped = og_pool.tile([P, 2, P, 4], BF16, align_bytes=64)
            bank = flip_psum.tile([P, BANK_PASSES, 2, P], F32)
            for gg in range(2):
                for u in range(2):
                    first = (2 * gg + u) * P
                    nc.tensor.transpose(bank[:, gg, u, :], pairs[:, first : first + P], ident[:])
            nc.scalar.copy(
                out=o_grouped[:].rearrange("p g s t -> p (g s t)").bitcast(F32).rearrange(
                    "p (g s u) -> p g s u", g=2, u=2
                ),
                in_=bank[:].rearrange("p g u s -> p g s u"),
            )
            og_of[j] = o_grouped

        def quantise_o(j):
            tok, half = pieces[j][1]
            groups = slice(2 * half, 2 * half + 2)
            nc.vector.quantize_mx(
                out=o_codes[:, tok, groups, :].rearrange("p g s -> p (g s)").bitcast(FP8X4),
                scales=o_scales[:, tok, groups, :].rearrange("p g s -> p (g s)"),
                in_=og_of[j][:].rearrange("p g s t -> p (g s t)"),
            )

        def project_out(blocks, on_vector):
            out_bank = acc_psum.tile([P, 2, X_COLS], F32, tag="acc")
            result = out_pool.tile([P, 2, X_COLS], F32)
            n = len(blocks)
            for b in range(n):
                tok, i = blocks[b]
                for g in range(K_GROUPS):
                    nc.tensor.matmul_mx(
                        out=out_bank[:, b, :],
                        lhsT=o_codes[:, tok, g, :].bitcast(FP8X4),
                        lhsT_scale=o_scales[:, tok, g, :],
                        rhs=x_codes[:, i, g, :].bitcast(FP8X4),
                        rhs_scale=x_scales[:, i, g, :],
                        start=(g == 0),
                        stop=(g == K_GROUPS - 1),
                    )
            if on_vector:
                nc.vector.tensor_copy(out=result[:, 0:n, :], in_=out_bank[:, 0:n, :])
            else:
                nc.scalar.copy(out=result[:, 0:n, :], in_=out_bank[:, 0:n, :])
            for b in range(n):
                tok, i = blocks[b]
                nc.sync.dma_start(
                    out=out[0, tok * P : (tok + 1) * P, i * X_COLS : (i + 1) * X_COLS],
                    in_=result[:, b, :],
                )

        for j in range(RAW_BUFS):
            load(j)
        sort_words(0)
        toks = []
        chunks = []
        waiting = []
        step = 0
        while step < count + 5 or waiting:
            j = step - 1
            if 0 <= j < count:
                quantise(j)
                if pieces[j][0] == "wo":
                    chunks.append(pieces[j][1])
                    waiting.extend([(tok, pieces[j][1]) for tok in toks])
            if 0 <= step < count:
                flip(step)
                if step + RAW_BUFS < count:
                    load(step + RAW_BUFS)
            if 0 <= step - 3 < count and pieces[step - 3][0] == "o_lat":
                flip_o(step - 3)
            if 0 <= step - 2 < count and pieces[step - 2][0] == "o_lat":
                up_project(step - 2)
            pairs = [waiting[:2], waiting[2:4]]
            if step >= count and len(waiting) <= 4:
                pairs = [waiting[:2], waiting[2:3], waiting[3:4]]
            for n in range(len(pairs)):
                if pairs[n]:
                    project_out(pairs[n], step >= count and n % 2 == 1)
                    for block in pairs[n]:
                        waiting.remove(block)
            if 0 <= step + 1 < count:
                sort_words(step + 1)
            if 0 <= step - 4 < count and pieces[step - 4][0] == "o_lat":
                quantise_o(step - 4)
                tok, half = pieces[step - 4][1]
                if half == 1:
                    toks.append(tok)
                    waiting.extend([(tok, i) for i in chunks])
            step += 1
